import numpy as np
import ml_dtypes


def mxq(x, axis, fmt="e4m3"):
    dtype, down = {"e4m3": (ml_dtypes.float8_e4m3fn, 7), "e5m2": (ml_dtypes.float8_e5m2, 14)}[fmt]
    v = np.moveaxis(np.asarray(x, np.float32).astype(ml_dtypes.bfloat16).astype(np.float64), axis, -1)
    blocks = v.reshape(v.shape[:-1] + (-1, 32))
    amax = np.abs(blocks).max(-1, keepdims=True)
    byte = np.maximum(np.where(amax > 0, np.frexp(amax)[1] - 1 + 127, 0) - down, 1)
    scale = np.exp2(byte - 127.0)
    codes = (blocks / scale).astype(np.float32).astype(dtype).astype(np.float64)
    return np.moveaxis((codes * scale).reshape(v.shape), -1, axis)


WIDE = False


def mx_kscale(k):
    if not WIDE:
        return np.ones(k)
    levels = np.array([10, -10, 5, -5, 0])
    if k % 512:
        return np.exp2(np.random.permutation(np.resize(levels, k // 32))).repeat(32)
    a = np.empty((k // 512, 16))
    for p in range(k // 512):
        a[p, :8] = np.random.permutation(np.resize(levels, 8))
        for g in range(8):
            far = levels[np.abs(levels - a[p, g]) >= 10]
            a[p, g + 8] = far[np.random.randint(len(far))]
    return np.exp2(a.ravel()).repeat(32)


BF16 = ml_dtypes.bfloat16


def bf(x):
    return np.asarray(x, np.float32).astype(BF16)


def f64(x):
    return np.asarray(x).astype(np.float64)


B, S, D, F = 2, 512, 2048, 2048
EPS = 1e-6


def setup_inputs():
    s = mx_kscale(D)
    p = np.exp2(np.round(np.log2(np.mean(1.0 / s**2)) / 2))
    q = np.exp2(np.round(np.log2(np.mean(s**2)) / 2))
    return {"x": bf(np.random.standard_normal((B, S, D)) * 0.5 * s * p),
            "weight": bf(np.random.standard_normal((F, D)) * 0.5 / s * q),
            "alpha": bf(1.0 + 0.1 * np.random.standard_normal(1)),
            "bias": bf(0.1 * np.random.standard_normal(F))}


def core(x, weight, alpha, bias):
    x = f64(x)
    weight = f64(weight)
    nf = weight.shape[0]
    y = mxq(x, 2, "e4m3") @ mxq(weight, 1, "e4m3").T
    x_sq = np.sum(x * x, axis=-1, keepdims=True)
    w_sq = np.sum(weight * weight, axis=-1)
    distances = x_sq + w_sq - 2.0 * y
    out = (y * y) / (distances + EPS)
    scale = (np.sqrt(nf) / np.log(1.0 + nf)) ** f64(alpha)
    out = out * scale + f64(bias)
    return out


def e4m3fn_bytes(y):
    return np.clip(np.asarray(y, np.float64), -448.0, 448.0).astype(np.float32).astype(ml_dtypes.float8_e4m3fn).view(np.uint8)


def reference(x, weight, alpha, bias):
    out = core(x, weight, alpha, bias)
    s = np.max(np.abs(out), axis=-1, keepdims=True) / 448.0
    return out, e4m3fn_bytes(out / s)

@@ -1,0 +1,358 @@
+import math
+from contextlib import ExitStack
+
+import concourse.masks as masks
+import concourse.mybir as mybir
+
+ROWS, K, F = 1024, 2048, 2048
+FLOPS = 2 * ROWS * K * F
+EPS = 1e-6
+
+F32 = mybir.dt.float32
+BF16 = mybir.dt.bfloat16
+U32 = mybir.dt.uint32
+U8 = mybir.dt.uint8
+FP8X4 = mybir.dt.float8_e4m3fn_x4
+FP8 = mybir.dt.float8_e4m3fn
+ACT = mybir.ActivationFunctionType
+ALU = mybir.AluOpType
+AX = mybir.AxisListType
+
+P = 128
+PASSES = K // 512
+N_TILE = 512
+CHUNKS = F // N_TILE
+ROW_TILES = ROWS // P
+W_TILES = F // P
+SQRT_C = math.sqrt(math.sqrt(F) / math.log(1.0 + F))
+
+GRAM_W = (1, 5, 9, 13)
+GRAM_X = (0, 1, 2, 3, 4, 5, 6, 7)
+W_SQ_ON_V = ()
+W_COPY_ON_S = (7,)
+GV = 0
+TAIL_GV = 1408
+W_BUFS = 5
+
+
+def tile_yatdense_kernel(tc, x, weight, alpha, bias, out_0, out_1):
+    nc = tc.nc
+    x_rows = x.flatten_outer_dims()
+    o0_rows = out_0.flatten_outer_dims()
+    o1_rows = out_1.flatten_outer_dims()
+
+    with ExitStack() as ctx:
+        keep = ctx.enter_context(tc.tile_pool(name="keep", bufs=1))
+        work = ctx.enter_context(tc.tile_pool(name="work", bufs=2))
+        psum = ctx.enter_context(tc.psum_pool(name="psum", bufs=8))
+
+        ident = keep.tile([P, P], F32)
+        masks.make_identity(nc, ident[:])
+        zeros = keep.tile([P, 1], F32)
+        nc.vector.memset(zeros[:], 0.0)
+        ones = keep.tile([P, 1], F32)
+        nc.vector.memset(ones[:], 1.0)
+
+        alpha_b = keep.tile([P, 1], BF16)
+        base = keep.tile([P, 1], F32)
+        warm = keep.tile([P, 1], F32)
+        sqrt_s = keep.tile([P, 1], F32)
+        w_codes = keep.tile([P, CHUNKS, PASSES, N_TILE], U32, align_bytes=64)
+        w_scales = keep.tile([P, CHUNKS, PASSES, N_TILE], U8, align_bytes=64)
+        x_codes = keep.tile([P, ROW_TILES, PASSES, P], U32, align_bytes=64)
+        x_scales = keep.tile([P, ROW_TILES, PASSES, P], U8, align_bytes=64)
+        wsq = keep.tile([P, W_TILES], F32)
+        xsq = keep.tile([P, ROW_TILES], F32)
+        wsq_b = keep.tile([P, F], F32)
+        bias_b = keep.tile([P, F], BF16)
+        amax = keep.tile([P, ROW_TILES], F32)
+        rmax = keep.tile([P, ROW_TILES], F32)
+        qscale = keep.tile([P, ROW_TILES], F32)
+        amax4 = keep.tile([P, CHUNKS], F32)
+
+        nat_w, nat_x, gws, gxs, tps, grams, accs, outs = {}, {}, {}, {}, {}, {}, {}, {}
+
+        def bank():
+            return psum.tile([P, 512], F32, tag="bank", name="bank")
+
+        def load_w(j):
+            nat_w[j] = work.tile([P, K], BF16, tag="natw", bufs=W_BUFS, name="natw")
+            nc.sync.dma_start(out=nat_w[j][:], in_=weight[j * P : (j + 1) * P, :])
+
+        def load_x(m):
+            nat_x[m] = work.tile([P, K], BF16, tag="natx", bufs=4, name="natx")
+            nc.sync.dma_start(out=nat_x[m][:], in_=x_rows[m * P : (m + 1) * P, :])
+
+        def squares_scalar(nat, dst):
+            junk = work.tile([P, K], BF16, tag="junk", name="junk")
+            nc.scalar.activation(out=junk[:], in_=nat[:], func=ACT.Square, accum_out=dst)
+
+        def squares_vector(nat, dst):
+            junkv = work.tile([P, K], BF16, tag="junkv", name="junkv", bufs=1)
+            nc.vector.scalar_tensor_tensor(
+                out=junkv[:], in0=nat[:], scalar=1.0, in1=nat[:], op0=ALU.mult, op1=ALU.mult, accum_out=dst
+            )
+
+        def turn(nat):
+            words = nat[:].bitcast(F32)
+            banks = []
+            for gp in range(PASSES // 2):
+                b = bank()
+                v = b[:].rearrange("p (g u r) -> p g u r", g=2, u=2)
+                for g2 in range(2):
+                    g = 2 * gp + g2
+                    for u in range(2):
+                        nc.tensor.transpose(v[:, g2, u, :], words[:, 256 * g + u : 256 * (g + 1) : 2], ident[:])
+                banks.append(b)
+            return banks
+
+        def copy_out(banks, grouped_words, on_vector):
+            for gp in range(PASSES // 2):
+                dst = grouped_words[:, 2 * gp : 2 * gp + 2, :, :]
+                src = banks[gp][:].rearrange("p (g u r) -> p g r u", g=2, u=2)
+                if on_vector:
+                    nc.vector.tensor_copy(out=dst, in_=src)
+                else:
+                    nc.scalar.copy(out=dst, in_=src)
+
+        def gram(grouped):
+            b = bank()
+            for g in range(PASSES):
+                for t in range(4):
+                    nc.tensor.matmul(
+                        out=b[:, 0:P],
+                        lhsT=grouped[:, g, :, t],
+                        rhs=grouped[:, g, :, t],
+                        start=(g == 0 and t == 0),
+                        stop=(g == PASSES - 1 and t == 3),
+                    )
+            return b
+
+        def diag(b, dst):
+            junkd = work.tile([P, P], F32, tag="junkd", name="junkd")
+            nc.vector.scalar_tensor_tensor(
+                out=junkd[:], in0=b[:, 0:P], scalar=1.0, in1=ident[:], op0=ALU.mult, op1=ALU.mult, accum_out=dst
+            )
+
+        def quantize_w(c):
+            for g in range(PASSES):
+                nc.vector.quantize_mx(
+                    out=w_codes[:, c, g, :].bitcast(FP8X4),
+                    scales=w_scales[:, c, g, :],
+                    in_=gws[c][:, g, :, :].rearrange("p f t -> p (f t)"),
+                )
+
+        def spread_wsq(c):
+            b = bank()
+            for jl in range(4):
+                j = 4 * c + jl
+                nc.tensor.transpose(b[:, jl * P : (jl + 1) * P], wsq[:, j : j + 1].to_broadcast([P, P]), ident[:])
+            nc.scalar.activation(out=wsq_b[:, c * N_TILE : (c + 1) * N_TILE], in_=b[:], func=ACT.Copy, bias=EPS)
+
+        def x_turn(m):
+            tps[m] = turn(nat_x[m])
+            if m not in GRAM_X:
+                squares_scalar(nat_x[m], xsq[:, m : m + 1])
+
+        def x_copy(m):
+            gxs[m] = work.tile([P, PASSES, P, 4], BF16, tag="gx", name="gx", bufs=3, align_bytes=64)
+            copy_out(tps[m], gxs[m][:].bitcast(F32), False)
+
+        def x_gram(m):
+            if m in GRAM_X:
+                grams[m] = gram(gxs[m])
+
+        def x_quant(m):
+            nc.vector.quantize_mx(
+                out=x_codes[:, m, :, :].rearrange("p g r -> p (g r)").bitcast(FP8X4),
+                scales=x_scales[:, m, :, :].rearrange("p g r -> p (g r)"),
+                in_=gxs[m][:].rearrange("p g r t -> p (g r t)"),
+            )
+
+        def x_diag(m):
+            if m in GRAM_X:
+                diag(grams[m], xsq[:, m : m + 1])
+
+        def mm(m, n):
+            accs[m, n] = bank()
+            for g in range(PASSES):
+                nc.tensor.matmul_mx(
+                    out=accs[m, n][:],
+                    lhsT=x_codes[:, m, g, :].bitcast(FP8X4),
+                    lhsT_scale=x_scales[:, m, g, :],
+                    rhs=w_codes[:, n, g, :].bitcast(FP8X4),
+                    rhs_scale=w_scales[:, n, g, :],
+                    start=(g == 0),
+                    stop=(g == PASSES - 1),
+                )
+
+        rss = {}
+
+        def dist_rsqrt(m, n):
+            cols = slice(n * N_TILE, (n + 1) * N_TILE)
+            dist = work.tile([P, N_TILE], F32, tag="dist", name="dist", bufs=3)
+            nc.vector.scalar_tensor_tensor(
+                out=dist[:], in0=accs[m, n][:], scalar=-2.0, in1=wsq_b[:, cols], op0=ALU.mult, op1=ALU.add
+            )
+            rss[m, n] = work.tile([P, N_TILE], F32, tag="rs", name="rs", bufs=5)
+            nc.scalar.activation(
+                out=rss[m, n][:], in_=dist[:], func=ACT.Abs_reciprocal_sqrt, bias=xsq[:, m : m + 1], scale=1.0
+            )
+
+        def finish(m, n, add=True):
+            cols = slice(n * N_TILE, (n + 1) * N_TILE)
+            if n == 0:
+                outs[m] = work.tile([P, F], F32, tag="o", name="o", bufs=4)
+            o = outs[m]
+            z = work.tile([P, N_TILE], F32, tag="z", name="z", bufs=3)
+            nc.vector.tensor_tensor(out=z[:], in0=accs[m, n][:], in1=rss[m, n][:], op=ALU.mult)
+            nc.scalar.activation(out=o[:, cols], in_=z[:], func=ACT.Square, scale=sqrt_s[:, 0:1])
+            if add:
+                nc.gpsimd.tensor_tensor(out=o[:, cols], in0=o[:, cols], in1=bias_b[:, cols], op=ALU.add)
+
+        def add_bias_vector(m, n):
+            cols = slice(n * N_TILE, (n + 1) * N_TILE)
+            nc.vector.tensor_tensor(out=outs[m][:, cols], in0=outs[m][:, cols], in1=bias_b[:, cols], op=ALU.add)
+
+        def row_max(m):
+            nc.vector.tensor_reduce(
+                out=amax[:, m : m + 1], in_=outs[m][:], axis=AX.X, op=ALU.max, apply_absolute_value=True
+            )
+
+        def part_max(m, n):
+            nc.vector.tensor_reduce(
+                out=amax4[:, n : n + 1], in_=outs[m][:, n * N_TILE : (n + 1) * N_TILE], axis=AX.X, op=ALU.max,
+                apply_absolute_value=True,
+            )
+
+        def join_max(m):
+            nc.vector.tensor_reduce(out=amax[:, m : m + 1], in_=amax4[:], axis=AX.X, op=ALU.max)
+
+        def invert_max(m):
+            nc.vector.reciprocal(out=rmax[:, m : m + 1], in_=amax[:, m : m + 1])
+
+        def scale_max(m):
+            nc.vector.tensor_scalar(
+                out=qscale[:, m : m + 1], in0=rmax[:, m : m + 1], scalar1=448.0, scalar2=None, op0=ALU.mult
+            )
+
+        def store_rows(m, lo, hi):
+            nc.sync.dma_start(out=o0_rows[m * P : (m + 1) * P, lo:hi], in_=outs[m][:, lo:hi])
+
+        def cast(m, gv):
+            o = outs[m]
+            q = work.tile([P, F], FP8, tag="q", name="q")
+            if gv > 0:
+                nc.vector.tensor_scalar(
+                    out=q[:, 0:gv], in0=o[:, 0:gv], scalar1=qscale[:, m : m + 1], scalar2=None, op0=ALU.mult,
+                    saturate=False,
+                )
+            nc.scalar.activation(
+                out=q[:, gv:F], in_=o[:, gv:F], func=ACT.Identity, scale=qscale[:, m : m + 1], bias=zeros[:, 0:1],
+                saturate=False,
+            )
+            nc.sync.dma_start(out=o1_rows[m * P : (m + 1) * P, :], in_=q[:].bitcast(U8))
+
+        with tc.manual_schedule():
+            nc.sync.dma_start(out=alpha_b[:], in_=alpha.partition_broadcast(P))
+            for j in range(W_BUFS):
+                load_w(j)
+            nc.scalar.activation(out=warm[:], in_=ones[:], func=ACT.Abs_reciprocal_sqrt)
+            nc.gpsimd.tensor_scalar(out=base[:], in0=ones[:], scalar1=SQRT_C, scalar2=0.0, op0=ALU.mult, op1=ALU.add)
+            nc.gpsimd.tensor_tensor(out=sqrt_s[:], in0=base[:], in1=alpha_b[:], op=ALU.pow)
+
+            wtp, wgram = {}, {}
+            for j in range(W_TILES + 4):
+                c, jl = divmod(j, 4)
+                i = j - W_TILES
+                if j < W_TILES:
+                    if jl == 0:
+                        gws[c] = work.tile([P, PASSES, N_TILE, 4], BF16, tag="gw", name="gw", align_bytes=64)
+                    wtp[j] = turn(nat_w[j])
+                    if j in GRAM_W:
+                        pass
+                    elif j in W_SQ_ON_V:
+                        squares_vector(nat_w[j], wsq[:, j : j + 1])
+                    else:
+                        squares_scalar(nat_w[j], wsq[:, j : j + 1])
+                elif i < 3:
+                    x_turn(i)
+                if j - 2 in GRAM_W:
+                    c2, jl2 = divmod(j - 2, 4)
+                    wgram[j - 2] = gram(gws[c2][:, :, jl2 * P : (jl2 + 1) * P, :])
+                if j < W_TILES:
+                    copy_out(wtp[j], gws[c][:].bitcast(F32)[:, :, jl * P : (jl + 1) * P, :], j not in W_COPY_ON_S)
+                elif i < 3:
+                    x_copy(i)
+                if j - 3 in GRAM_W:
+                    diag(wgram[j - 3], wsq[:, j - 3 : j - 2])
+                if 1 <= i:
+                    x_gram(i - 1)
+                if jl == 1 and c > 0:
+                    quantize_w(c - 1)
+                if i == 2 or i == 3:
+                    x_quant(i - 2)
+                if 2 <= i:
+                    x_diag(i - 2)
+                if jl == 3 and c > 0:
+                    spread_wsq(c - 1)
+                if j + W_BUFS < W_TILES:
+                    load_w(j + W_BUFS)
+                if j in (4, 6, 10, 12):
+                    load_x((4, 6, 10, 12).index(j))
+                if j == 8:
+                    nc.sync.dma_start(out=bias_b[:], in_=bias.partition_broadcast(P))
+            for n in range(CHUNKS):
+                mm(0, n)
+            x_diag(2)
+
+            last = ROW_TILES - 1
+            for m in range(ROW_TILES):
+                nxt = m + 1 < ROW_TILES
+                pre = m + 3 < ROW_TILES
+                if m + 4 < ROW_TILES:
+                    load_x(m + 4)
+                if pre:
+                    x_turn(m + 3)
+                if nxt:
+                    mm(m + 1, 0)
+                    mm(m + 1, 1)
+                for n in range(CHUNKS):
+                    dist_rsqrt(m, n)
+                if m + 2 < ROW_TILES:
+                    x_quant(m + 2)
+                if pre:
+                    x_copy(m + 3)
+                finish(m, 0)
+                finish(m, 1)
+                if m == last:
+                    store_rows(m, 0, F // 2)
+                if pre:
+                    x_gram(m + 3)
+                if nxt:
+                    mm(m + 1, 2)
+                    mm(m + 1, 3)
+                if m >= 1:
+                    row_max(m - 1)
+                    store_rows(m - 1, 0, F)
+                if m >= 2:
+                    cast(m - 2, GV)
+                finish(m, 2)
+                if m >= 1:
+                    invert_max(m - 1)
+                finish(m, 3, m != last)
+                if m >= 1:
+                    scale_max(m - 1)
+                if pre:
+                    x_diag(m + 3)
+            cast(last - 1, GV)
+            part_max(last, 0)
+            part_max(last, 1)
+            add_bias_vector(last, 3)
+            store_rows(last, F // 2, F)
+            part_max(last, 2)
+            part_max(last, 3)
+            join_max(last)
+            invert_max(last)
+            scale_max(last)
+            cast(last, TAIL_GV)

@@ -147,7 +147,9 @@ def tile_yatdense_kernel(tc, x, weight, alpha, bias, out_0, out_1):
             for jl in range(4):
                 j = 4 * c + jl
                 nc.tensor.transpose(b[:, jl * P : (jl + 1) * P], wsq[:, j : j + 1].to_broadcast([P, P]), ident[:])
-            nc.scalar.activation(out=wsq_b[:, c * N_TILE : (c + 1) * N_TILE], in_=b[:], func=ACT.Copy, bias=EPS)
+            nc.vector.tensor_scalar(
+                out=wsq_b[:, c * N_TILE : (c + 1) * N_TILE], in0=b[:], scalar1=EPS, scalar2=None, op0=ALU.add
+            )
 
         def x_turn(m):
             tps[m] = turn(nat_x[m])

@@ -29,10 +29,11 @@ SQRT_C = math.sqrt(math.sqrt(F) / math.log(1.0 + F))
 GRAM_W = (1, 5, 9, 13)
 GRAM_X = (0, 1, 2, 3, 4, 5, 6, 7)
 W_SQ_ON_V = ()
-W_COPY_ON_S = (7,)
+W_SQ_ON_G = (4, 12)
+W_COPY_ON_S = (3, 7, 11)
 GV = 0
 TAIL_GV = 1408
-W_BUFS = 5
+W_BUFS = 6
 
 
 def tile_yatdense_kernel(tc, x, weight, alpha, bias, out_0, out_1):
@@ -93,6 +94,32 @@ def tile_yatdense_kernel(tc, x, weight, alpha, bias, out_0, out_1):
                 out=junkv[:], in0=nat[:], scalar=1.0, in1=nat[:], op0=ALU.mult, op1=ALU.mult, accum_out=dst
             )
 
+        sqgs = {}
+
+        def squares_gpsimd(j):
+            sqgs[j] = work.tile([P, K], F32, tag="sqg", name="sqg", bufs=1)
+            sq = sqgs[j]
+            for lo in range(0, K, N_TILE):
+                nc.gpsimd.tensor_tensor(
+                    out=sq[:, lo : lo + N_TILE], in0=nat_w[j][:, lo : lo + N_TILE], in1=nat_w[j][:, lo : lo + N_TILE],
+                    op=ALU.mult,
+                )
+            for lo in range(0, K // 2, N_TILE):
+                nc.gpsimd.tensor_tensor(
+                    out=sq[:, lo : lo + N_TILE], in0=sq[:, lo : lo + N_TILE],
+                    in1=sq[:, K // 2 + lo : K // 2 + lo + N_TILE], op=ALU.add,
+                )
+            width = K // 4
+            for k in range(8):
+                if width >= 128:
+                    nc.gpsimd.tensor_tensor(
+                        out=sq[:, 0:width], in0=sq[:, 0:width], in1=sq[:, width : 2 * width], op=ALU.add
+                    )
+                    width = width // 2
+
+        def squares_gpsimd_end(j):
+            nc.vector.tensor_reduce(out=wsq[:, j : j + 1], in_=sqgs[j][:, 0:128], axis=AX.X, op=ALU.add)
+
         def turn(nat):
             words = nat[:].bitcast(F32)
             banks = []
@@ -147,9 +174,7 @@ def tile_yatdense_kernel(tc, x, weight, alpha, bias, out_0, out_1):
             for jl in range(4):
                 j = 4 * c + jl
                 nc.tensor.transpose(b[:, jl * P : (jl + 1) * P], wsq[:, j : j + 1].to_broadcast([P, P]), ident[:])
-            nc.vector.tensor_scalar(
-                out=wsq_b[:, c * N_TILE : (c + 1) * N_TILE], in0=b[:], scalar1=EPS, scalar2=None, op0=ALU.add
-            )
+            nc.scalar.activation(out=wsq_b[:, c * N_TILE : (c + 1) * N_TILE], in_=b[:], func=ACT.Copy, bias=EPS)
 
         def x_turn(m):
             tps[m] = turn(nat_x[m])
@@ -273,6 +298,8 @@ def tile_yatdense_kernel(tc, x, weight, alpha, bias, out_0, out_1):
                     wtp[j] = turn(nat_w[j])
                     if j in GRAM_W:
                         pass
+                    elif j in W_SQ_ON_G:
+                        squares_gpsimd(j)
                     elif j in W_SQ_ON_V:
                         squares_vector(nat_w[j], wsq[:, j : j + 1])
                     else:
@@ -296,6 +323,8 @@ def tile_yatdense_kernel(tc, x, weight, alpha, bias, out_0, out_1):
                     x_quant(i - 2)
                 if 2 <= i:
                     x_diag(i - 2)
+                if j - 6 in W_SQ_ON_G:
+                    squares_gpsimd_end(j - 6)
                 if jl == 3 and c > 0:
                     spread_wsq(c - 1)
                 if j + W_BUFS < W_TILES:

@@ -268,7 +268,7 @@ def tile_yatdense_kernel(tc, x, weight, alpha, bias, out_0, out_1):
 
         def cast(m, gv):
             o = outs[m]
-            q = work.tile([P, F], FP8, tag="q", name="q")
+            q = work.tile([P, F], FP8, tag="q", name="q", bufs=3)
             if gv > 0:
                 nc.vector.tensor_scalar(
                     out=q[:, 0:gv], in0=o[:, 0:gv], scalar1=qscale[:, m : m + 1], scalar2=None, op0=ALU.mult,
@@ -356,8 +356,6 @@ def tile_yatdense_kernel(tc, x, weight, alpha, bias, out_0, out_1):
                     x_copy(m + 3)
                 finish(m, 0)
                 finish(m, 1)
-                if m == last:
-                    store_rows(m, 0, F // 2)
                 if pre:
                     x_gram(m + 3)
                 if nxt:
@@ -368,6 +366,8 @@ def tile_yatdense_kernel(tc, x, weight, alpha, bias, out_0, out_1):
                     store_rows(m - 1, 0, F)
                 if m >= 2:
                     cast(m - 2, GV)
+                if m == last:
+                    store_rows(m, 0, F // 2)
                 finish(m, 2)
                 if m >= 1:
                     invert_max(m - 1)

@@ -162,11 +162,11 @@ def tile_yatdense_kernel(tc, x, weight, alpha, bias, out_0, out_1):
             )
 
         def quantize_w(c):
-            for g in range(PASSES):
+            for h in range(PASSES // 2):
                 nc.vector.quantize_mx(
-                    out=w_codes[:, c, g, :].bitcast(FP8X4),
-                    scales=w_scales[:, c, g, :],
-                    in_=gws[c][:, g, :, :].rearrange("p f t -> p (f t)"),
+                    out=w_codes[:, c, 2 * h : 2 * h + 2, :].rearrange("p g f -> p (g f)").bitcast(FP8X4),
+                    scales=w_scales[:, c, 2 * h : 2 * h + 2, :].rearrange("p g f -> p (g f)"),
+                    in_=gws[c][:, 2 * h : 2 * h + 2, :, :].rearrange("p g f t -> p (g f t)"),
                 )
 
         def spread_wsq(c):
@@ -281,12 +281,9 @@ def tile_yatdense_kernel(tc, x, weight, alpha, bias, out_0, out_1):
             nc.sync.dma_start(out=o1_rows[m * P : (m + 1) * P, :], in_=q[:].bitcast(U8))
 
         with tc.manual_schedule():
-            nc.sync.dma_start(out=alpha_b[:], in_=alpha.partition_broadcast(P))
             for j in range(W_BUFS):
                 load_w(j)
             nc.scalar.activation(out=warm[:], in_=ones[:], func=ACT.Abs_reciprocal_sqrt)
-            nc.gpsimd.tensor_scalar(out=base[:], in0=ones[:], scalar1=SQRT_C, scalar2=0.0, op0=ALU.mult, op1=ALU.add)
-            nc.gpsimd.tensor_tensor(out=sqrt_s[:], in0=base[:], in1=alpha_b[:], op=ALU.pow)
 
             wtp, wgram = {}, {}
             for j in range(W_TILES + 4):
@@ -333,6 +330,12 @@ def tile_yatdense_kernel(tc, x, weight, alpha, bias, out_0, out_1):
                     load_x((4, 6, 10, 12).index(j))
                 if j == 8:
                     nc.sync.dma_start(out=bias_b[:], in_=bias.partition_broadcast(P))
+                    nc.sync.dma_start(out=alpha_b[:], in_=alpha.partition_broadcast(P))
+                if j == 13:
+                    nc.gpsimd.tensor_scalar(
+                        out=base[:], in0=ones[:], scalar1=SQRT_C, scalar2=0.0, op0=ALU.mult, op1=ALU.add
+                    )
+                    nc.gpsimd.tensor_tensor(out=sqrt_s[:], in0=base[:], in1=alpha_b[:], op=ALU.pow)
             for n in range(CHUNKS):
                 mm(0, n)
             x_diag(2)

@@ -24,7 +24,7 @@ N_TILE = 512
 CHUNKS = F // N_TILE
 ROW_TILES = ROWS // P
 W_TILES = F // P
-SQRT_C = math.sqrt(math.sqrt(F) / math.log(1.0 + F))
+INV_C = math.log(1.0 + F) / math.sqrt(F)
 
 GRAM_W = (1, 5, 9, 13)
 GRAM_X = (0, 1, 2, 3, 4, 5, 6, 7)
@@ -34,6 +34,7 @@ W_COPY_ON_S = (3, 7, 11)
 GV = 0
 TAIL_GV = 1408
 W_BUFS = 6
+SQUARE_ON_G = (0,)
 
 
 def tile_yatdense_kernel(tc, x, weight, alpha, bias, out_0, out_1):
@@ -57,7 +58,8 @@ def tile_yatdense_kernel(tc, x, weight, alpha, bias, out_0, out_1):
         alpha_b = keep.tile([P, 1], BF16)
         base = keep.tile([P, 1], F32)
         warm = keep.tile([P, 1], F32)
-        sqrt_s = keep.tile([P, 1], F32)
+        inv_s = keep.tile([P, 1], F32)
+        xsq_s = keep.tile([P, ROW_TILES], F32)
         w_codes = keep.tile([P, CHUNKS, PASSES, N_TILE], U32, align_bytes=64)
         w_scales = keep.tile([P, CHUNKS, PASSES, N_TILE], U8, align_bytes=64)
         x_codes = keep.tile([P, ROW_TILES, PASSES, P], U32, align_bytes=64)
@@ -199,6 +201,7 @@ def tile_yatdense_kernel(tc, x, weight, alpha, bias, out_0, out_1):
         def x_diag(m):
             if m in GRAM_X:
                 diag(grams[m], xsq[:, m : m + 1])
+            nc.gpsimd.tensor_tensor(out=xsq_s[:, m : m + 1], in0=xsq[:, m : m + 1], in1=inv_s[:], op=ALU.mult)
 
         def mm(m, n):
             accs[m, n] = bank()
@@ -223,7 +226,7 @@ def tile_yatdense_kernel(tc, x, weight, alpha, bias, out_0, out_1):
             )
             rss[m, n] = work.tile([P, N_TILE], F32, tag="rs", name="rs", bufs=5)
             nc.scalar.activation(
-                out=rss[m, n][:], in_=dist[:], func=ACT.Abs_reciprocal_sqrt, bias=xsq[:, m : m + 1], scale=1.0
+                out=rss[m, n][:], in_=dist[:], func=ACT.Abs_reciprocal_sqrt, bias=xsq_s[:, m : m + 1], scale=inv_s[:, 0:1]
             )
 
         def finish(m, n, add=True):
@@ -233,7 +236,10 @@ def tile_yatdense_kernel(tc, x, weight, alpha, bias, out_0, out_1):
             o = outs[m]
             z = work.tile([P, N_TILE], F32, tag="z", name="z", bufs=3)
             nc.vector.tensor_tensor(out=z[:], in0=accs[m, n][:], in1=rss[m, n][:], op=ALU.mult)
-            nc.scalar.activation(out=o[:, cols], in_=z[:], func=ACT.Square, scale=sqrt_s[:, 0:1])
+            if n in SQUARE_ON_G and add:
+                nc.gpsimd.tensor_tensor(out=o[:, cols], in0=z[:], in1=z[:], op=ALU.mult)
+            else:
+                nc.scalar.activation(out=o[:, cols], in_=z[:], func=ACT.Square)
             if add:
                 nc.gpsimd.tensor_tensor(out=o[:, cols], in0=o[:, cols], in1=bias_b[:, cols], op=ALU.add)
 
@@ -333,9 +339,9 @@ def tile_yatdense_kernel(tc, x, weight, alpha, bias, out_0, out_1):
                     nc.sync.dma_start(out=alpha_b[:], in_=alpha.partition_broadcast(P))
                 if j == 13:
                     nc.gpsimd.tensor_scalar(
-                        out=base[:], in0=ones[:], scalar1=SQRT_C, scalar2=0.0, op0=ALU.mult, op1=ALU.add
+                        out=base[:], in0=ones[:], scalar1=INV_C, scalar2=0.0, op0=ALU.mult, op1=ALU.add
                     )
-                    nc.gpsimd.tensor_tensor(out=sqrt_s[:], in0=base[:], in1=alpha_b[:], op=ALU.pow)
+                    nc.gpsimd.tensor_tensor(out=inv_s[:], in0=base[:], in1=alpha_b[:], op=ALU.pow)
             for n in range(CHUNKS):
                 mm(0, n)
             x_diag(2)

@@ -284,7 +284,11 @@ def tile_yatdense_kernel(tc, x, weight, alpha, bias, out_0, out_1):
                 out=q[:, gv:F], in_=o[:, gv:F], func=ACT.Identity, scale=qscale[:, m : m + 1], bias=zeros[:, 0:1],
                 saturate=False,
             )
-            nc.sync.dma_start(out=o1_rows[m * P : (m + 1) * P, :], in_=q[:].bitcast(U8))
+            if gv > 0:
+                nc.sync.dma_start(out=o1_rows[m * P : (m + 1) * P, gv:F], in_=q[:, gv:F].bitcast(U8))
+                nc.sync.dma_start(out=o1_rows[m * P : (m + 1) * P, 0:gv], in_=q[:, 0:gv].bitcast(U8))
+            else:
+                nc.sync.dma_start(out=o1_rows[m * P : (m + 1) * P, :], in_=q[:].bitcast(U8))
 
         with tc.manual_schedule():
             for j in range(W_BUFS):
@@ -328,8 +332,8 @@ def tile_yatdense_kernel(tc, x, weight, alpha, bias, out_0, out_1):
                     x_diag(i - 2)
                 if j - 6 in W_SQ_ON_G:
                     squares_gpsimd_end(j - 6)
-                if jl == 3 and c > 0:
-                    spread_wsq(c - 1)
+                if (jl == 1 and c > 1) or j == W_TILES + 3:
+                    spread_wsq(c - 2 if jl == 1 else CHUNKS - 1)
                 if j + W_BUFS < W_TILES:
                     load_w(j + W_BUFS)
                 if j in (4, 6, 10, 12):
@@ -388,8 +392,9 @@ def tile_yatdense_kernel(tc, x, weight, alpha, bias, out_0, out_1):
             cast(last - 1, GV)
             part_max(last, 0)
             part_max(last, 1)
+            store_rows(last, F // 2, 3 * F // 4)
             add_bias_vector(last, 3)
-            store_rows(last, F // 2, F)
+            store_rows(last, 3 * F // 4, F)
             part_max(last, 2)
             part_max(last, 3)
             join_max(last)

@@ -26,15 +26,16 @@ ROW_TILES = ROWS // P
 W_TILES = F // P
 INV_C = math.log(1.0 + F) / math.sqrt(F)
 
-GRAM_W = (1, 5, 9, 13)
+GRAM_W = (5, 6, 12, 13)
 GRAM_X = (0, 1, 2, 3, 4, 5, 6, 7)
 W_SQ_ON_V = ()
-W_SQ_ON_G = (4, 12)
+W_SQ_ON_G = (0, 8)
 W_COPY_ON_S = (3, 7, 11)
 GV = 0
 TAIL_GV = 1408
 W_BUFS = 6
 SQUARE_ON_G = (0,)
+G_LAG = 6
 
 
 def tile_yatdense_kernel(tc, x, weight, alpha, bias, out_0, out_1):
@@ -296,7 +297,7 @@ def tile_yatdense_kernel(tc, x, weight, alpha, bias, out_0, out_1):
             nc.scalar.activation(out=warm[:], in_=ones[:], func=ACT.Abs_reciprocal_sqrt)
 
             wtp, wgram = {}, {}
-            for j in range(W_TILES + 4):
+            for j in range(W_TILES + 3):
                 c, jl = divmod(j, 4)
                 i = j - W_TILES
                 if j < W_TILES:
@@ -311,14 +312,14 @@ def tile_yatdense_kernel(tc, x, weight, alpha, bias, out_0, out_1):
                         squares_vector(nat_w[j], wsq[:, j : j + 1])
                     else:
                         squares_scalar(nat_w[j], wsq[:, j : j + 1])
-                elif i < 3:
+                elif i < 2:
                     x_turn(i)
                 if j - 2 in GRAM_W:
                     c2, jl2 = divmod(j - 2, 4)
                     wgram[j - 2] = gram(gws[c2][:, :, jl2 * P : (jl2 + 1) * P, :])
                 if j < W_TILES:
                     copy_out(wtp[j], gws[c][:].bitcast(F32)[:, :, jl * P : (jl + 1) * P, :], j not in W_COPY_ON_S)
-                elif i < 3:
+                elif i < 2:
                     x_copy(i)
                 if j - 3 in GRAM_W:
                     diag(wgram[j - 3], wsq[:, j - 3 : j - 2])
@@ -326,13 +327,13 @@ def tile_yatdense_kernel(tc, x, weight, alpha, bias, out_0, out_1):
                     x_gram(i - 1)
                 if jl == 1 and c > 0:
                     quantize_w(c - 1)
-                if i == 2 or i == 3:
-                    x_quant(i - 2)
+                if i == 1 or i == 2:
+                    x_quant(i - 1)
                 if 2 <= i:
                     x_diag(i - 2)
-                if j - 6 in W_SQ_ON_G:
-                    squares_gpsimd_end(j - 6)
-                if (jl == 1 and c > 1) or j == W_TILES + 3:
+                if j - G_LAG in W_SQ_ON_G:
+                    squares_gpsimd_end(j - G_LAG)
+                if (jl == 1 and c > 1) or j == W_TILES + 2:
                     spread_wsq(c - 2 if jl == 1 else CHUNKS - 1)
                 if j + W_BUFS < W_TILES:
                     load_w(j + W_BUFS)
@@ -348,29 +349,27 @@ def tile_yatdense_kernel(tc, x, weight, alpha, bias, out_0, out_1):
                     nc.gpsimd.tensor_tensor(out=inv_s[:], in0=base[:], in1=alpha_b[:], op=ALU.pow)
             for n in range(CHUNKS):
                 mm(0, n)
-            x_diag(2)
+            x_diag(1)
 
             last = ROW_TILES - 1
             for m in range(ROW_TILES):
                 nxt = m + 1 < ROW_TILES
-                pre = m + 3 < ROW_TILES
+                pre = m + 2 < ROW_TILES
                 if m + 4 < ROW_TILES:
                     load_x(m + 4)
                 if pre:
-                    x_turn(m + 3)
+                    x_turn(m + 2)
                 if nxt:
                     mm(m + 1, 0)
                     mm(m + 1, 1)
                 for n in range(CHUNKS):
                     dist_rsqrt(m, n)
-                if m + 2 < ROW_TILES:
-                    x_quant(m + 2)
                 if pre:
-                    x_copy(m + 3)
+                    x_copy(m + 2)
                 finish(m, 0)
                 finish(m, 1)
                 if pre:
-                    x_gram(m + 3)
+                    x_gram(m + 2)
                 if nxt:
                     mm(m + 1, 2)
                     mm(m + 1, 3)
@@ -381,6 +380,8 @@ def tile_yatdense_kernel(tc, x, weight, alpha, bias, out_0, out_1):
                     cast(m - 2, GV)
                 if m == last:
                     store_rows(m, 0, F // 2)
+                if pre:
+                    x_quant(m + 2)
                 finish(m, 2)
                 if m >= 1:
                     invert_max(m - 1)
@@ -388,7 +389,7 @@ def tile_yatdense_kernel(tc, x, weight, alpha, bias, out_0, out_1):
                 if m >= 1:
                     scale_max(m - 1)
                 if pre:
-                    x_diag(m + 3)
+                    x_diag(m + 2)
             cast(last - 1, GV)
             part_max(last, 0)
             part_max(last, 1)

@@ -26,11 +26,11 @@ ROW_TILES = ROWS // P
 W_TILES = F // P
 INV_C = math.log(1.0 + F) / math.sqrt(F)
 
-GRAM_W = (5, 6, 12, 13)
+GRAM_W = (5, 13)
 GRAM_X = (0, 1, 2, 3, 4, 5, 6, 7)
 W_SQ_ON_V = ()
 W_SQ_ON_G = (0, 8)
-W_COPY_ON_S = (3, 7, 11)
+W_COPY_ON_S = ()
 GV = 0
 TAIL_GV = 1408
 W_BUFS = 6

@@ -27,7 +27,7 @@ W_TILES = F // P
 INV_C = math.log(1.0 + F) / math.sqrt(F)
 
 GRAM_W = (5, 13)
-GRAM_X = (0, 1, 2, 3, 4, 5, 6, 7)
+GRAM_X = (0, 1, 4, 5, 6, 7)
 W_SQ_ON_V = ()
 W_SQ_ON_G = (0, 8)
 W_COPY_ON_S = ()
@@ -36,6 +36,7 @@ TAIL_GV = 1408
 W_BUFS = 6
 SQUARE_ON_G = (0,)
 G_LAG = 6
+X_SQ_EARLY = {17: 2, 18: 3}
 
 
 def tile_yatdense_kernel(tc, x, weight, alpha, bias, out_0, out_1):
@@ -181,7 +182,7 @@ def tile_yatdense_kernel(tc, x, weight, alpha, bias, out_0, out_1):
 
         def x_turn(m):
             tps[m] = turn(nat_x[m])
-            if m not in GRAM_X:
+            if m not in GRAM_X and m not in X_SQ_EARLY.values():
                 squares_scalar(nat_x[m], xsq[:, m : m + 1])
 
         def x_copy(m):
@@ -321,6 +322,8 @@ def tile_yatdense_kernel(tc, x, weight, alpha, bias, out_0, out_1):
                     copy_out(wtp[j], gws[c][:].bitcast(F32)[:, :, jl * P : (jl + 1) * P, :], j not in W_COPY_ON_S)
                 elif i < 2:
                     x_copy(i)
+                if j in X_SQ_EARLY:
+                    squares_scalar(nat_x[X_SQ_EARLY[j]], xsq[:, X_SQ_EARLY[j] : X_SQ_EARLY[j] + 1])
                 if j - 3 in GRAM_W:
                     diag(wgram[j - 3], wsq[:, j - 3 : j - 2])
                 if 1 <= i:

import math
from contextlib import ExitStack

import concourse.masks as masks
import concourse.mybir as mybir

ROWS, K, F = 1024, 2048, 2048
FLOPS = 2 * ROWS * K * F
EPS = 1e-6

F32 = mybir.dt.float32
BF16 = mybir.dt.bfloat16
U32 = mybir.dt.uint32
U8 = mybir.dt.uint8
FP8X4 = mybir.dt.float8_e4m3fn_x4
FP8 = mybir.dt.float8_e4m3fn
ACT = mybir.ActivationFunctionType
ALU = mybir.AluOpType
AX = mybir.AxisListType

P = 128
PASSES = K // 512
N_TILE = 512
CHUNKS = F // N_TILE
ROW_TILES = ROWS // P
W_TILES = F // P
INV_C = math.log(1.0 + F) / math.sqrt(F)

GRAM_W = (5, 13)
GRAM_X = (0, 1, 4, 5, 6, 7)
W_SQ_ON_V = ()
W_SQ_ON_G = (0, 8)
W_COPY_ON_S = ()
GV = 0
TAIL_GV = 1408
W_BUFS = 6
SQUARE_ON_G = (0,)
G_LAG = 6
X_SQ_EARLY = {17: 2, 18: 3}


def tile_yatdense_kernel(tc, x, weight, alpha, bias, out_0, out_1):
    nc = tc.nc
    x_rows = x.flatten_outer_dims()
    o0_rows = out_0.flatten_outer_dims()
    o1_rows = out_1.flatten_outer_dims()

    with ExitStack() as ctx:
        keep = ctx.enter_context(tc.tile_pool(name="keep", bufs=1))
        work = ctx.enter_context(tc.tile_pool(name="work", bufs=2))
        psum = ctx.enter_context(tc.psum_pool(name="psum", bufs=8))

        ident = keep.tile([P, P], F32)
        masks.make_identity(nc, ident[:])
        zeros = keep.tile([P, 1], F32)
        nc.vector.memset(zeros[:], 0.0)
        ones = keep.tile([P, 1], F32)
        nc.vector.memset(ones[:], 1.0)

        alpha_b = keep.tile([P, 1], BF16)
        base = keep.tile([P, 1], F32)
        warm = keep.tile([P, 1], F32)
        inv_s = keep.tile([P, 1], F32)
        xsq_s = keep.tile([P, ROW_TILES], F32)
        w_codes = keep.tile([P, CHUNKS, PASSES, N_TILE], U32, align_bytes=64)
        w_scales = keep.tile([P, CHUNKS, PASSES, N_TILE], U8, align_bytes=64)
        x_codes = keep.tile([P, ROW_TILES, PASSES, P], U32, align_bytes=64)
        x_scales = keep.tile([P, ROW_TILES, PASSES, P], U8, align_bytes=64)
        wsq = keep.tile([P, W_TILES], F32)
        xsq = keep.tile([P, ROW_TILES], F32)
        wsq_b = keep.tile([P, F], F32)
        bias_b = keep.tile([P, F], BF16)
        amax = keep.tile([P, ROW_TILES], F32)
        rmax = keep.tile([P, ROW_TILES], F32)
        qscale = keep.tile([P, ROW_TILES], F32)
        amax4 = keep.tile([P, CHUNKS], F32)

        nat_w, nat_x, gws, gxs, tps, grams, accs, outs = {}, {}, {}, {}, {}, {}, {}, {}

        def bank():
            return psum.tile([P, 512], F32, tag="bank", name="bank")

        def load_w(j):
            nat_w[j] = work.tile([P, K], BF16, tag="natw", bufs=W_BUFS, name="natw")
            nc.sync.dma_start(out=nat_w[j][:], in_=weight[j * P : (j + 1) * P, :])

        def load_x(m):
            nat_x[m] = work.tile([P, K], BF16, tag="natx", bufs=4, name="natx")
            nc.sync.dma_start(out=nat_x[m][:], in_=x_rows[m * P : (m + 1) * P, :])

        def squares_scalar(nat, dst):
            junk = work.tile([P, K], BF16, tag="junk", name="junk")
            nc.scalar.activation(out=junk[:], in_=nat[:], func=ACT.Square, accum_out=dst)

        def squares_vector(nat, dst):
            junkv = work.tile([P, K], BF16, tag="junkv", name="junkv", bufs=1)
            nc.vector.scalar_tensor_tensor(
                out=junkv[:], in0=nat[:], scalar=1.0, in1=nat[:], op0=ALU.mult, op1=ALU.mult, accum_out=dst
            )

        sqgs = {}

        def squares_gpsimd(j):
            sqgs[j] = work.tile([P, K], F32, tag="sqg", name="sqg", bufs=1)
            sq = sqgs[j]
            for lo in range(0, K, N_TILE):
                nc.gpsimd.tensor_tensor(
                    out=sq[:, lo : lo + N_TILE], in0=nat_w[j][:, lo : lo + N_TILE], in1=nat_w[j][:, lo : lo + N_TILE],
                    op=ALU.mult,
                )
            for lo in range(0, K // 2, N_TILE):
                nc.gpsimd.tensor_tensor(
                    out=sq[:, lo : lo + N_TILE], in0=sq[:, lo : lo + N_TILE],
                    in1=sq[:, K // 2 + lo : K // 2 + lo + N_TILE], op=ALU.add,
                )
            width = K // 4
            for k in range(8):
                if width >= 128:
                    nc.gpsimd.tensor_tensor(
                        out=sq[:, 0:width], in0=sq[:, 0:width], in1=sq[:, width : 2 * width], op=ALU.add
                    )
                    width = width // 2

        def squares_gpsimd_end(j):
            nc.vector.tensor_reduce(out=wsq[:, j : j + 1], in_=sqgs[j][:, 0:128], axis=AX.X, op=ALU.add)

        def turn(nat):
            words = nat[:].bitcast(F32)
            banks = []
            for gp in range(PASSES // 2):
                b = bank()
                v = b[:].rearrange("p (g u r) -> p g u r", g=2, u=2)
                for g2 in range(2):
                    g = 2 * gp + g2
                    for u in range(2):
                        nc.tensor.transpose(v[:, g2, u, :], words[:, 256 * g + u : 256 * (g + 1) : 2], ident[:])
                banks.append(b)
            return banks

        def copy_out(banks, grouped_words, on_vector):
            for gp in range(PASSES // 2):
                dst = grouped_words[:, 2 * gp : 2 * gp + 2, :, :]
                src = banks[gp][:].rearrange("p (g u r) -> p g r u", g=2, u=2)
                if on_vector:
                    nc.vector.tensor_copy(out=dst, in_=src)
                else:
                    nc.scalar.copy(out=dst, in_=src)

        def gram(grouped):
            b = bank()
            for g in range(PASSES):
                for t in range(4):
                    nc.tensor.matmul(
                        out=b[:, 0:P],
                        lhsT=grouped[:, g, :, t],
                        rhs=grouped[:, g, :, t],
                        start=(g == 0 and t == 0),
                        stop=(g == PASSES - 1 and t == 3),
                    )
            return b

        def diag(b, dst):
            junkd = work.tile([P, P], F32, tag="junkd", name="junkd")
            nc.vector.scalar_tensor_tensor(
                out=junkd[:], in0=b[:, 0:P], scalar=1.0, in1=ident[:], op0=ALU.mult, op1=ALU.mult, accum_out=dst
            )

        def quantize_w(c):
            for h in range(PASSES // 2):
                nc.vector.quantize_mx(
                    out=w_codes[:, c, 2 * h : 2 * h + 2, :].rearrange("p g f -> p (g f)").bitcast(FP8X4),
                    scales=w_scales[:, c, 2 * h : 2 * h + 2, :].rearrange("p g f -> p (g f)"),
                    in_=gws[c][:, 2 * h : 2 * h + 2, :, :].rearrange("p g f t -> p (g f t)"),
                )

        def spread_wsq(c):
            b = bank()
            for jl in range(4):
                j = 4 * c + jl
                nc.tensor.transpose(b[:, jl * P : (jl + 1) * P], wsq[:, j : j + 1].to_broadcast([P, P]), ident[:])
            nc.scalar.activation(out=wsq_b[:, c * N_TILE : (c + 1) * N_TILE], in_=b[:], func=ACT.Copy, bias=EPS)

        def x_turn(m):
            tps[m] = turn(nat_x[m])
            if m not in GRAM_X and m not in X_SQ_EARLY.values():
                squares_scalar(nat_x[m], xsq[:, m : m + 1])

        def x_copy(m):
            gxs[m] = work.tile([P, PASSES, P, 4], BF16, tag="gx", name="gx", bufs=3, align_bytes=64)
            copy_out(tps[m], gxs[m][:].bitcast(F32), False)

        def x_gram(m):
            if m in GRAM_X:
                grams[m] = gram(gxs[m])

        def x_quant(m):
            nc.vector.quantize_mx(
                out=x_codes[:, m, :, :].rearrange("p g r -> p (g r)").bitcast(FP8X4),
                scales=x_scales[:, m, :, :].rearrange("p g r -> p (g r)"),
                in_=gxs[m][:].rearrange("p g r t -> p (g r t)"),
            )

        def x_diag(m):
            if m in GRAM_X:
                diag(grams[m], xsq[:, m : m + 1])
            nc.gpsimd.tensor_tensor(out=xsq_s[:, m : m + 1], in0=xsq[:, m : m + 1], in1=inv_s[:], op=ALU.mult)

        def mm(m, n):
            accs[m, n] = bank()
            for g in range(PASSES):
                nc.tensor.matmul_mx(
                    out=accs[m, n][:],
                    lhsT=x_codes[:, m, g, :].bitcast(FP8X4),
                    lhsT_scale=x_scales[:, m, g, :],
                    rhs=w_codes[:, n, g, :].bitcast(FP8X4),
                    rhs_scale=w_scales[:, n, g, :],
                    start=(g == 0),
                    stop=(g == PASSES - 1),
                )

        rss = {}

        def dist_rsqrt(m, n):
            cols = slice(n * N_TILE, (n + 1) * N_TILE)
            dist = work.tile([P, N_TILE], F32, tag="dist", name="dist", bufs=3)
            nc.vector.scalar_tensor_tensor(
                out=dist[:], in0=accs[m, n][:], scalar=-2.0, in1=wsq_b[:, cols], op0=ALU.mult, op1=ALU.add
            )
            rss[m, n] = work.tile([P, N_TILE], F32, tag="rs", name="rs", bufs=5)
            nc.scalar.activation(
                out=rss[m, n][:], in_=dist[:], func=ACT.Abs_reciprocal_sqrt, bias=xsq_s[:, m : m + 1], scale=inv_s[:, 0:1]
            )

        def finish(m, n, add=True):
            cols = slice(n * N_TILE, (n + 1) * N_TILE)
            if n == 0:
                outs[m] = work.tile([P, F], F32, tag="o", name="o", bufs=4)
            o = outs[m]
            z = work.tile([P, N_TILE], F32, tag="z", name="z", bufs=3)
            nc.vector.tensor_tensor(out=z[:], in0=accs[m, n][:], in1=rss[m, n][:], op=ALU.mult)
            if n in SQUARE_ON_G and add:
                nc.gpsimd.tensor_tensor(out=o[:, cols], in0=z[:], in1=z[:], op=ALU.mult)
            else:
                nc.scalar.activation(out=o[:, cols], in_=z[:], func=ACT.Square)
            if add:
                nc.gpsimd.tensor_tensor(out=o[:, cols], in0=o[:, cols], in1=bias_b[:, cols], op=ALU.add)

        def add_bias_vector(m, n):
            cols = slice(n * N_TILE, (n + 1) * N_TILE)
            nc.vector.tensor_tensor(out=outs[m][:, cols], in0=outs[m][:, cols], in1=bias_b[:, cols], op=ALU.add)

        def row_max(m):
            nc.vector.tensor_reduce(
                out=amax[:, m : m + 1], in_=outs[m][:], axis=AX.X, op=ALU.max, apply_absolute_value=True
            )

        def part_max(m, n):
            nc.vector.tensor_reduce(
                out=amax4[:, n : n + 1], in_=outs[m][:, n * N_TILE : (n + 1) * N_TILE], axis=AX.X, op=ALU.max,
                apply_absolute_value=True,
            )

        def join_max(m):
            nc.vector.tensor_reduce(out=amax[:, m : m + 1], in_=amax4[:], axis=AX.X, op=ALU.max)

        def invert_max(m):
            nc.vector.reciprocal(out=rmax[:, m : m + 1], in_=amax[:, m : m + 1])

        def scale_max(m):
            nc.vector.tensor_scalar(
                out=qscale[:, m : m + 1], in0=rmax[:, m : m + 1], scalar1=448.0, scalar2=None, op0=ALU.mult
            )

        def store_rows(m, lo, hi):
            nc.sync.dma_start(out=o0_rows[m * P : (m + 1) * P, lo:hi], in_=outs[m][:, lo:hi])

        def cast(m, gv):
            o = outs[m]
            q = work.tile([P, F], FP8, tag="q", name="q", bufs=3)
            if gv > 0:
                nc.vector.tensor_scalar(
                    out=q[:, 0:gv], in0=o[:, 0:gv], scalar1=qscale[:, m : m + 1], scalar2=None, op0=ALU.mult,
                    saturate=False,
                )
            nc.scalar.activation(
                out=q[:, gv:F], in_=o[:, gv:F], func=ACT.Identity, scale=qscale[:, m : m + 1], bias=zeros[:, 0:1],
                saturate=False,
            )
            if gv > 0:
                nc.sync.dma_start(out=o1_rows[m * P : (m + 1) * P, gv:F], in_=q[:, gv:F].bitcast(U8))
                nc.sync.dma_start(out=o1_rows[m * P : (m + 1) * P, 0:gv], in_=q[:, 0:gv].bitcast(U8))
            else:
                nc.sync.dma_start(out=o1_rows[m * P : (m + 1) * P, :], in_=q[:].bitcast(U8))

        with tc.manual_schedule():
            for j in range(W_BUFS):
                load_w(j)
            nc.scalar.activation(out=warm[:], in_=ones[:], func=ACT.Abs_reciprocal_sqrt)

            wtp, wgram = {}, {}
            for j in range(W_TILES + 3):
                c, jl = divmod(j, 4)
                i = j - W_TILES
                if j < W_TILES:
                    if jl == 0:
                        gws[c] = work.tile([P, PASSES, N_TILE, 4], BF16, tag="gw", name="gw", align_bytes=64)
                    wtp[j] = turn(nat_w[j])
                    if j in GRAM_W:
                        pass
                    elif j in W_SQ_ON_G:
                        squares_gpsimd(j)
                    elif j in W_SQ_ON_V:
                        squares_vector(nat_w[j], wsq[:, j : j + 1])
                    else:
                        squares_scalar(nat_w[j], wsq[:, j : j + 1])
                elif i < 2:
                    x_turn(i)
                if j - 2 in GRAM_W:
                    c2, jl2 = divmod(j - 2, 4)
                    wgram[j - 2] = gram(gws[c2][:, :, jl2 * P : (jl2 + 1) * P, :])
                if j < W_TILES:
                    copy_out(wtp[j], gws[c][:].bitcast(F32)[:, :, jl * P : (jl + 1) * P, :], j not in W_COPY_ON_S)
                elif i < 2:
                    x_copy(i)
                if j in X_SQ_EARLY:
                    squares_scalar(nat_x[X_SQ_EARLY[j]], xsq[:, X_SQ_EARLY[j] : X_SQ_EARLY[j] + 1])
                if j - 3 in GRAM_W:
                    diag(wgram[j - 3], wsq[:, j - 3 : j - 2])
                if 1 <= i:
                    x_gram(i - 1)
                if jl == 1 and c > 0:
                    quantize_w(c - 1)
                if i == 1 or i == 2:
                    x_quant(i - 1)
                if 2 <= i:
                    x_diag(i - 2)
                if j - G_LAG in W_SQ_ON_G:
                    squares_gpsimd_end(j - G_LAG)
                if (jl == 1 and c > 1) or j == W_TILES + 2:
                    spread_wsq(c - 2 if jl == 1 else CHUNKS - 1)
                if j + W_BUFS < W_TILES:
                    load_w(j + W_BUFS)
                if j in (4, 6, 10, 12):
                    load_x((4, 6, 10, 12).index(j))
                if j == 8:
                    nc.sync.dma_start(out=bias_b[:], in_=bias.partition_broadcast(P))
                    nc.sync.dma_start(out=alpha_b[:], in_=alpha.partition_broadcast(P))
                if j == 13:
                    nc.gpsimd.tensor_scalar(
                        out=base[:], in0=ones[:], scalar1=INV_C, scalar2=0.0, op0=ALU.mult, op1=ALU.add
                    )
                    nc.gpsimd.tensor_tensor(out=inv_s[:], in0=base[:], in1=alpha_b[:], op=ALU.pow)
            for n in range(CHUNKS):
                mm(0, n)
            x_diag(1)

            last = ROW_TILES - 1
            for m in range(ROW_TILES):
                nxt = m + 1 < ROW_TILES
                pre = m + 2 < ROW_TILES
                if m + 4 < ROW_TILES:
                    load_x(m + 4)
                if pre:
                    x_turn(m + 2)
                if nxt:
                    mm(m + 1, 0)
                    mm(m + 1, 1)
                for n in range(CHUNKS):
                    dist_rsqrt(m, n)
                if pre:
                    x_copy(m + 2)
                finish(m, 0)
                finish(m, 1)
                if pre:
                    x_gram(m + 2)
                if nxt:
                    mm(m + 1, 2)
                    mm(m + 1, 3)
                if m >= 1:
                    row_max(m - 1)
                    store_rows(m - 1, 0, F)
                if m >= 2:
                    cast(m - 2, GV)
                if m == last:
                    store_rows(m, 0, F // 2)
                if pre:
                    x_quant(m + 2)
                finish(m, 2)
                if m >= 1:
                    invert_max(m - 1)
                finish(m, 3, m != last)
                if m >= 1:
                    scale_max(m - 1)
                if pre:
                    x_diag(m + 2)
            cast(last - 1, GV)
            part_max(last, 0)
            part_max(last, 1)
            store_rows(last, F // 2, 3 * F // 4)
            add_bias_vector(last, 3)
            store_rows(last, 3 * F // 4, F)
            part_max(last, 2)
            part_max(last, 3)
            join_max(last)
            invert_max(last)
            scale_max(last)
            cast(last, TAIL_GV)
